import numpy as np
import ml_dtypes


def mxq(x, axis, fmt="e4m3"):
    dtype, down = {"e4m3": (ml_dtypes.float8_e4m3fn, 7), "e5m2": (ml_dtypes.float8_e5m2, 14)}[fmt]
    v = np.moveaxis(np.asarray(x, np.float32).astype(ml_dtypes.bfloat16).astype(np.float64), axis, -1)
    blocks = v.reshape(v.shape[:-1] + (-1, 32))
    amax = np.abs(blocks).max(-1, keepdims=True)
    byte = np.maximum(np.where(amax > 0, np.frexp(amax)[1] - 1 + 127, 0) - down, 1)
    scale = np.exp2(byte - 127.0)
    codes = (blocks / scale).astype(np.float32).astype(dtype).astype(np.float64)
    return np.moveaxis((codes * scale).reshape(v.shape), -1, axis)


WIDE = False


def mx_kscale(k):
    if not WIDE:
        return np.ones(k)
    levels = np.array([10, -10, 5, -5, 0])
    a = np.random.permutation(np.resize(levels, k // 512 * 4)).reshape(k // 512, 4)
    idx = np.arange(k)
    return np.exp2(a[idx // 512, idx % 128 // 32])


BF16 = ml_dtypes.bfloat16


def bf(x):
    return np.asarray(x, np.float32).astype(BF16)


def f64(x):
    return np.asarray(x).astype(np.float64)


B, T, E, C, H, XB = 1, 512, 2048, 2048, 16, 512
D = C // H
EPS = 1e-5


def silu(a):
    return a / (1.0 + np.exp(-a))


def setup_inputs():
    s, t = mx_kscale(E), mx_kscale(C)
    amp = 2.0 ** np.linspace(-8.0, 2.0, H)
    y = np.random.standard_normal((B, T, H, D)) * amp[None, None, :, None]
    return {"x": bf(np.random.standard_normal((B, T, E)) * s),
            "y_ret": bf(y.reshape(B, T, C)),
            "w_g": bf(np.random.standard_normal((E, C)) / np.sqrt(E) / s[:, None]),
            "w_proj": bf(np.random.standard_normal((C, E)) / np.sqrt(C) / t[:, None]),
            "gn_weight": bf((1.0 + 0.1 * np.random.standard_normal(C)) * t),
            "gn_bias": bf(0.1 * np.random.standard_normal(C) * t)}


def reference(x, y_ret, w_g, w_proj, gn_weight, gn_bias):
    yg = f64(y_ret).reshape(B * T, H, D)
    mu = yg.mean(axis=-1, keepdims=True)
    var = yg.var(axis=-1, keepdims=True)
    yn = (yg - mu) / np.sqrt(var + EPS)
    yn = yn.reshape(B * T, C) * f64(gn_weight)[None] + f64(gn_bias)[None]
    yn = yn.reshape(B, T, C)
    g = mxq(f64(x), 2, "e4m3") @ mxq(f64(w_g), 0, "e4m3")
    h = silu(g) * yn
    return mxq(h, 2, "e4m3") @ mxq(f64(w_proj), 0, "e4m3")

@@ -1,0 +1,255 @@
+from contextlib import ExitStack
+
+import concourse.mybir as mybir
+from concourse.masks import make_identity
+
+F32 = mybir.dt.float32
+BF16 = mybir.dt.bfloat16
+U32 = mybir.dt.uint32
+U8 = mybir.dt.uint8
+FP8X4 = mybir.dt.float8_e4m3fn_x4
+ACT = mybir.ActivationFunctionType
+ALU = mybir.AluOpType
+
+P = 128
+PACK = 4
+K_PASS = P * PACK
+TOKENS = 512
+WIDTH = 2048
+HEADS = 16
+HEAD_DIM = 128
+EPS = 1e-5
+PASSES = WIDTH // K_PASS
+TOKEN_TILES = TOKENS // P
+BANK = 512
+CHUNK_COLS = 1024
+HALVES = WIDTH // CHUNK_COLS
+N_CHUNKS = 2 * HALVES * PASSES
+PREFETCH = 3
+RUN = 4
+VECTOR_COLS = 640
+
+FLOPS = 2 * 2 * TOKENS * WIDTH * WIDTH
+
+
+def tile_multiscaleretention_pc_kernel(tc, x, y_ret, w_g, w_proj, gn_weight, gn_bias, out):
+    nc = tc.nc
+    x_rows = x.rearrange("b t e -> (b t) e")
+    y_rows = y_ret.rearrange("b t c -> (b t) c")
+    out_rows = out.rearrange("b t e -> (b t) e")
+
+    with ExitStack() as ctx:
+        const = ctx.enter_context(tc.tile_pool(name="const", bufs=1))
+        raw_pool = ctx.enter_context(tc.tile_pool(name="raw", bufs=5))
+        grouped_pool = ctx.enter_context(tc.tile_pool(name="grouped", bufs=3))
+        act_grouped_pool = ctx.enter_context(tc.tile_pool(name="act_grouped", bufs=2))
+        weight_codes_pool = ctx.enter_context(tc.tile_pool(name="weight_codes", bufs=12))
+        z_pool = ctx.enter_context(tc.tile_pool(name="z", bufs=4))
+        gate_pool = ctx.enter_context(tc.tile_pool(name="gate", bufs=2))
+        out_pool = ctx.enter_context(tc.tile_pool(name="out_stage", bufs=6))
+        psum = ctx.enter_context(tc.psum_pool(name="psum", bufs=8))
+
+        y_sb = const.tile([P, TOKEN_TILES, WIDTH], BF16)
+        for tt in range(TOKEN_TILES):
+            nc.sync.dma_start(out=y_sb[:, tt, :], in_=y_rows[tt * P : (tt + 1) * P, :])
+        x_sb = []
+        for pair in range(TOKEN_TILES // 2):
+            x_pair = raw_pool.tile([P, 2, WIDTH], BF16, name="x_pair", tag="raw")
+            nc.sync.dma_start(
+                out=x_pair[:],
+                in_=x_rows[pair * 2 * P : (pair + 1) * 2 * P, :].rearrange("(s p) e -> p s e", p=P),
+            )
+            x_sb.append(x_pair)
+
+        raw_chunks = {}
+
+        def load_chunk(n):
+            raw = raw_pool.tile([P, PACK, CHUNK_COLS], BF16, name="raw", tag="raw")
+            half, k_pass = (n % 8) // PASSES, n % PASSES
+            rows = slice(k_pass * K_PASS, (k_pass + 1) * K_PASS)
+            cols = slice(half * CHUNK_COLS, (half + 1) * CHUNK_COLS)
+            if n < 8:
+                for u in range(2):
+                    part = slice(k_pass * K_PASS + u * 2 * P, k_pass * K_PASS + (u + 1) * 2 * P)
+                    nc.sync.dma_start(
+                        out=raw[:, 2 * u : 2 * u + 2, :],
+                        in_=w_g[part, cols].rearrange("(q e) c -> q e c", e=2),
+                    )
+            else:
+                nc.sync.dma_start(out=raw[:], in_=w_proj[rows, cols].rearrange("(j p) n -> p j n", p=P))
+            raw_chunks[n] = raw
+
+        for n in range(PREFETCH):
+            load_chunk(n)
+
+        ident = const.tile([P, P], F32)
+        make_identity(nc, ident[:])
+
+        gain_rows = const.tile([P, P], BF16)
+        nc.vector.memset(gain_rows[:], 0.0)
+        nc.scalar.dma_start(out=gain_rows[0:HEADS, :], in_=gn_weight.rearrange("(h c) -> h c", c=HEAD_DIM))
+        nc.scalar.dma_start(out=gain_rows[HEADS : 2 * HEADS, :], in_=gn_bias.rearrange("(h c) -> h c", c=HEAD_DIM))
+        gain_rows_f32 = const.tile([P, P], F32)
+        nc.vector.tensor_copy(out=gain_rows_f32[:], in_=gain_rows[:])
+        gain_bank = psum.tile([P, BANK], F32, name="gain_bank", tag="bank")
+        nc.tensor.transpose(gain_bank[:, 0:P], gain_rows_f32[:], ident[:])
+        gain_cols = const.tile([P, 2 * HEADS], F32)
+        nc.vector.tensor_copy(out=gain_cols[:], in_=gain_bank[:, 0 : 2 * HEADS])
+
+        groups = TOKEN_TILES * HEADS
+        stats = const.tile([P, groups, 6], F32)
+        for tt in range(TOKEN_TILES):
+            for h in range(HEADS):
+                nc.vector.bn_stats(out=stats[:, tt * HEADS + h, :], in_=y_sb[:, tt, h * HEAD_DIM : (h + 1) * HEAD_DIM])
+        mean_even, m2_even = stats[:, :, 1], stats[:, :, 2]
+        mean_odd, m2_odd = stats[:, :, 4], stats[:, :, 5]
+        mean = const.tile([P, groups], F32)
+        gap = const.tile([P, groups], F32)
+        var = const.tile([P, groups], F32)
+        std = const.tile([P, groups], F32)
+        rstd = const.tile([P, groups], F32)
+        nc.vector.tensor_tensor(out=mean[:], in0=mean_even, in1=mean_odd, op=ALU.add)
+        nc.vector.tensor_scalar_mul(out=mean[:], in0=mean[:], scalar1=0.5)
+        nc.vector.tensor_tensor(out=gap[:], in0=mean_even, in1=mean_odd, op=ALU.subtract)
+        nc.vector.tensor_tensor(out=gap[:], in0=gap[:], in1=gap[:], op=ALU.mult)
+        nc.vector.tensor_tensor(out=var[:], in0=m2_even, in1=m2_odd, op=ALU.add)
+        nc.vector.tensor_scalar(out=var[:], in0=var[:], scalar1=1.0 / HEAD_DIM, scalar2=EPS, op0=ALU.mult, op1=ALU.add)
+        nc.vector.scalar_tensor_tensor(out=var[:], in0=gap[:], scalar=0.25, in1=var[:], op0=ALU.mult, op1=ALU.add)
+        nc.scalar.activation(out=std[:], in_=var[:], func=ACT.Sqrt)
+        nc.vector.reciprocal(out=rstd[:], in_=std[:])
+
+        x_codes = const.tile([P, PASSES, TOKENS], U32, align_bytes=64)
+        x_scales = const.tile([P, PASSES, TOKENS], U8, align_bytes=64)
+        for g in range(PASSES):
+            x_grouped = act_grouped_pool.tile([P, TOKENS, PACK], BF16, name="x_grouped", tag="act_grouped", align_bytes=64)
+            x_words = x_grouped[:].rearrange("p w t -> p (w t)").bitcast(F32).rearrange("p (w u) -> p w u", u=2)
+            for pair in range(TOKEN_TILES // 2):
+                xt = psum.tile([P, 2, 2 * P], F32, name="xt", tag="bank")
+                for s in range(2):
+                    words = x_sb[pair][:, s, :].bitcast(F32)
+                    for u in range(2):
+                        first = g * 2 * P + u * P
+                        nc.tensor.transpose(xt[:, u, s * P : (s + 1) * P], words[:, first : first + P], ident[:])
+                nc.scalar.copy(out=x_words[:, pair * 2 * P : (pair + 1) * 2 * P, :], in_=xt[:].rearrange("p u w -> p w u"))
+            nc.vector.quantize_mx(
+                out=x_codes[:, g, :].bitcast(FP8X4),
+                scales=x_scales[:, g, :],
+                in_=x_grouped[:].rearrange("p w t -> p (w t)"),
+            )
+
+        weight_codes = {}
+        weight_scales = {}
+
+        def prepare_chunk(n):
+            raw = raw_chunks[n]
+            grouped = grouped_pool.tile([P, CHUNK_COLS, PACK], BF16, name="grouped", tag="grouped", align_bytes=64)
+            dst = grouped[:].rearrange("p (c i) t -> p c t i", i=RUN)
+            src = raw[:].rearrange("p t (c i) -> p c t i", i=RUN)
+            split = VECTOR_COLS // RUN
+            nc.vector.tensor_copy(out=dst[:, :split], in_=src[:, :split])
+            nc.scalar.copy(out=dst[:, split:], in_=src[:, split:])
+            codes = weight_codes_pool.tile([P, CHUNK_COLS], U32, name="codes", tag="codes", align_bytes=64)
+            scales = weight_codes_pool.tile([P, CHUNK_COLS], U8, name="scales", tag="scales", align_bytes=64)
+            nc.vector.quantize_mx(
+                out=codes[:].bitcast(FP8X4), scales=scales[:], in_=grouped[:].rearrange("p w t -> p (w t)")
+            )
+            weight_codes[n] = codes
+            weight_scales[n] = scales
+
+        normed = {}
+
+        def normalise(group):
+            yn = gate_pool.tile([P, PACK, TOKENS], F32, name="yn", tag="yn")
+            for j in range(PACK):
+                h = group * PACK + j
+                z = z_pool.tile([P, TOKEN_TILES, HEAD_DIM], F32, name="z", tag="z")
+                for tt in range(TOKEN_TILES):
+                    col = tt * HEADS + h
+                    nc.vector.tensor_scalar(
+                        out=z[:, tt, :],
+                        in0=y_sb[:, tt, h * HEAD_DIM : (h + 1) * HEAD_DIM],
+                        scalar1=mean[:, col : col + 1],
+                        scalar2=rstd[:, col : col + 1],
+                        op0=ALU.subtract,
+                        op1=ALU.mult,
+                    )
+                zt = psum.tile([P, BANK], F32, name="zt", tag="bank")
+                for tt in range(TOKEN_TILES):
+                    nc.tensor.transpose(zt[:, tt * P : (tt + 1) * P], z[:, tt, :], ident[:])
+                nc.scalar.activation(
+                    out=yn[:, j, :],
+                    in_=zt[:],
+                    func=ACT.Identity,
+                    scale=gain_cols[:, h : h + 1],
+                    bias=gain_cols[:, HEADS + h : HEADS + h + 1],
+                )
+            normed[group] = yn
+
+        h_codes = const.tile([P, PASSES, TOKENS], U32, align_bytes=64)
+        h_scales = const.tile([P, PASSES, TOKENS], U8, align_bytes=64)
+
+        def gate(group):
+            silu = gate_pool.tile([P, PACK, TOKENS], F32, name="silu", tag="silu")
+            for j in range(PACK):
+                c_tile = group * PACK + j
+                half = c_tile * P // CHUNK_COLS
+                cols = slice(c_tile * P - half * CHUNK_COLS, (c_tile + 1) * P - half * CHUNK_COLS)
+                acc = psum.tile([P, BANK], F32, name="acc", tag="bank")
+                for g in range(PASSES):
+                    n = half * PASSES + g
+                    nc.tensor.matmul_mx(
+                        out=acc[:],
+                        lhsT=weight_codes[n][:, cols].bitcast(FP8X4),
+                        lhsT_scale=weight_scales[n][:, cols],
+                        rhs=x_codes[:, g, :].bitcast(FP8X4),
+                        rhs_scale=x_scales[:, g, :],
+                        start=(g == 0),
+                        stop=(g == PASSES - 1),
+                    )
+                nc.scalar.activation(out=silu[:, j, :], in_=acc[:], func=ACT.Silu)
+            h_grouped = act_grouped_pool.tile([P, TOKENS, PACK], BF16, name="h_grouped", tag="act_grouped", align_bytes=64)
+            nc.vector.tensor_tensor(
+                out=h_grouped[:].rearrange("p (c i) t -> p c t i", i=RUN),
+                in0=silu[:].rearrange("p t (c i) -> p c t i", i=RUN),
+                in1=normed[group][:].rearrange("p t (c i) -> p c t i", i=RUN),
+                op=ALU.mult,
+            )
+            nc.vector.quantize_mx(
+                out=h_codes[:, group, :].bitcast(FP8X4),
+                scales=h_scales[:, group, :],
+                in_=h_grouped[:].rearrange("p w t -> p (w t)"),
+            )
+
+        def project(m):
+            half = m * BANK // CHUNK_COLS
+            cols = slice(m * BANK - half * CHUNK_COLS, (m + 1) * BANK - half * CHUNK_COLS)
+            for tt in range(TOKEN_TILES):
+                acc = psum.tile([P, BANK], F32, name="acc2", tag="bank")
+                for group in range(PASSES):
+                    n = 8 + half * PASSES + group
+                    nc.tensor.matmul_mx(
+                        out=acc[:],
+                        lhsT=h_codes[:, group, tt * P : (tt + 1) * P].bitcast(FP8X4),
+                        lhsT_scale=h_scales[:, group, tt * P : (tt + 1) * P],
+                        rhs=weight_codes[n][:, cols].bitcast(FP8X4),
+                        rhs_scale=weight_scales[n][:, cols],
+                        start=(group == 0),
+                        stop=(group == PASSES - 1),
+                    )
+                stage = out_pool.tile([P, BANK], F32, name="stage", tag="stage")
+                nc.scalar.copy(out=stage[:], in_=acc[:])
+                nc.sync.dma_start(out=out_rows[tt * P : (tt + 1) * P, m * BANK : (m + 1) * BANK], in_=stage[:])
+
+        for n in range(N_CHUNKS):
+            if n + PREFETCH < N_CHUNKS:
+                load_chunk(n + PREFETCH)
+            prepare_chunk(n)
+            if n % 2 == 1:
+                step = n // 2
+                if step < PASSES:
+                    normalise(step)
+                if 1 <= step <= PASSES:
+                    gate(step - 1)
+                if step > PASSES:
+                    project(step - PASSES - 1)
+        project(PASSES - 1)

@@ -27,7 +27,7 @@ HALVES = WIDTH // CHUNK_COLS
 N_CHUNKS = 2 * HALVES * PASSES
 PREFETCH = 3
 RUN = 4
-VECTOR_COLS = 640
+VECTOR_COLS = 512
 
 FLOPS = 2 * 2 * TOKENS * WIDTH * WIDTH
 
@@ -43,23 +43,12 @@ def tile_multiscaleretention_pc_kernel(tc, x, y_ret, w_g, w_proj, gn_weight, gn_
         raw_pool = ctx.enter_context(tc.tile_pool(name="raw", bufs=5))
         grouped_pool = ctx.enter_context(tc.tile_pool(name="grouped", bufs=3))
         act_grouped_pool = ctx.enter_context(tc.tile_pool(name="act_grouped", bufs=2))
-        weight_codes_pool = ctx.enter_context(tc.tile_pool(name="weight_codes", bufs=12))
+        weight_codes_pool = ctx.enter_context(tc.tile_pool(name="weight_codes", bufs=10))
         z_pool = ctx.enter_context(tc.tile_pool(name="z", bufs=4))
-        gate_pool = ctx.enter_context(tc.tile_pool(name="gate", bufs=2))
-        out_pool = ctx.enter_context(tc.tile_pool(name="out_stage", bufs=6))
+        yn_pool = ctx.enter_context(tc.tile_pool(name="yn", bufs=4))
+        silu_pool = ctx.enter_context(tc.tile_pool(name="silu", bufs=2))
+        out_pool = ctx.enter_context(tc.tile_pool(name="out_stage", bufs=4))
         psum = ctx.enter_context(tc.psum_pool(name="psum", bufs=8))
-
-        y_sb = const.tile([P, TOKEN_TILES, WIDTH], BF16)
-        for tt in range(TOKEN_TILES):
-            nc.sync.dma_start(out=y_sb[:, tt, :], in_=y_rows[tt * P : (tt + 1) * P, :])
-        x_sb = []
-        for pair in range(TOKEN_TILES // 2):
-            x_pair = raw_pool.tile([P, 2, WIDTH], BF16, name="x_pair", tag="raw")
-            nc.sync.dma_start(
-                out=x_pair[:],
-                in_=x_rows[pair * 2 * P : (pair + 1) * 2 * P, :].rearrange("(s p) e -> p s e", p=P),
-            )
-            x_sb.append(x_pair)
 
         raw_chunks = {}
 
@@ -79,8 +68,19 @@ def tile_multiscaleretention_pc_kernel(tc, x, y_ret, w_g, w_proj, gn_weight, gn_
                 nc.sync.dma_start(out=raw[:], in_=w_proj[rows, cols].rearrange("(j p) n -> p j n", p=P))
             raw_chunks[n] = raw
 
-        for n in range(PREFETCH):
-            load_chunk(n)
+        y_sb = const.tile([P, TOKEN_TILES, WIDTH], BF16)
+        for tt in range(TOKEN_TILES):
+            nc.sync.dma_start(out=y_sb[:, tt, :], in_=y_rows[tt * P : (tt + 1) * P, :])
+            if tt < PREFETCH:
+                load_chunk(tt)
+        x_sb = []
+        for pair in range(TOKEN_TILES // 2):
+            x_pair = raw_pool.tile([P, 2, WIDTH], BF16, name="x_pair", tag="raw")
+            nc.sync.dma_start(
+                out=x_pair[:],
+                in_=x_rows[pair * 2 * P : (pair + 1) * 2 * P, :].rearrange("(s p) e -> p s e", p=P),
+            )
+            x_sb.append(x_pair)
 
         ident = const.tile([P, P], F32)
         make_identity(nc, ident[:])
@@ -98,9 +98,11 @@ def tile_multiscaleretention_pc_kernel(tc, x, y_ret, w_g, w_proj, gn_weight, gn_
 
         groups = TOKEN_TILES * HEADS
         stats = const.tile([P, groups, 6], F32)
-        for tt in range(TOKEN_TILES):
+
+        def take_statistics(tt):
             for h in range(HEADS):
                 nc.vector.bn_stats(out=stats[:, tt * HEADS + h, :], in_=y_sb[:, tt, h * HEAD_DIM : (h + 1) * HEAD_DIM])
+
         mean_even, m2_even = stats[:, :, 1], stats[:, :, 2]
         mean_odd, m2_odd = stats[:, :, 4], stats[:, :, 5]
         mean = const.tile([P, groups], F32)
@@ -108,50 +110,67 @@ def tile_multiscaleretention_pc_kernel(tc, x, y_ret, w_g, w_proj, gn_weight, gn_
         var = const.tile([P, groups], F32)
         std = const.tile([P, groups], F32)
         rstd = const.tile([P, groups], F32)
-        nc.vector.tensor_tensor(out=mean[:], in0=mean_even, in1=mean_odd, op=ALU.add)
-        nc.vector.tensor_scalar_mul(out=mean[:], in0=mean[:], scalar1=0.5)
-        nc.vector.tensor_tensor(out=gap[:], in0=mean_even, in1=mean_odd, op=ALU.subtract)
-        nc.vector.tensor_tensor(out=gap[:], in0=gap[:], in1=gap[:], op=ALU.mult)
-        nc.vector.tensor_tensor(out=var[:], in0=m2_even, in1=m2_odd, op=ALU.add)
-        nc.vector.tensor_scalar(out=var[:], in0=var[:], scalar1=1.0 / HEAD_DIM, scalar2=EPS, op0=ALU.mult, op1=ALU.add)
-        nc.vector.scalar_tensor_tensor(out=var[:], in0=gap[:], scalar=0.25, in1=var[:], op0=ALU.mult, op1=ALU.add)
-        nc.scalar.activation(out=std[:], in_=var[:], func=ACT.Sqrt)
-        nc.vector.reciprocal(out=rstd[:], in_=std[:])
+
+        def join_statistics():
+            nc.vector.tensor_tensor(out=mean[:], in0=mean_even, in1=mean_odd, op=ALU.add)
+            nc.vector.tensor_scalar_mul(out=mean[:], in0=mean[:], scalar1=0.5)
+            nc.vector.tensor_tensor(out=gap[:], in0=mean_even, in1=mean_odd, op=ALU.subtract)
+            nc.vector.tensor_tensor(out=gap[:], in0=gap[:], in1=gap[:], op=ALU.mult)
+            nc.vector.tensor_tensor(out=var[:], in0=m2_even, in1=m2_odd, op=ALU.add)
+            nc.vector.tensor_scalar(
+                out=var[:], in0=var[:], scalar1=1.0 / HEAD_DIM, scalar2=EPS, op0=ALU.mult, op1=ALU.add
+            )
+            nc.vector.scalar_tensor_tensor(out=var[:], in0=gap[:], scalar=0.25, in1=var[:], op0=ALU.mult, op1=ALU.add)
+            nc.scalar.activation(out=std[:], in_=var[:], func=ACT.Sqrt)
+            nc.vector.reciprocal(out=rstd[:], in_=std[:])
 
         x_codes = const.tile([P, PASSES, TOKENS], U32, align_bytes=64)
         x_scales = const.tile([P, PASSES, TOKENS], U8, align_bytes=64)
-        for g in range(PASSES):
-            x_grouped = act_grouped_pool.tile([P, TOKENS, PACK], BF16, name="x_grouped", tag="act_grouped", align_bytes=64)
-            x_words = x_grouped[:].rearrange("p w t -> p (w t)").bitcast(F32).rearrange("p (w u) -> p w u", u=2)
-            for pair in range(TOKEN_TILES // 2):
-                xt = psum.tile([P, 2, 2 * P], F32, name="xt", tag="bank")
-                for s in range(2):
-                    words = x_sb[pair][:, s, :].bitcast(F32)
-                    for u in range(2):
-                        first = g * 2 * P + u * P
-                        nc.tensor.transpose(xt[:, u, s * P : (s + 1) * P], words[:, first : first + P], ident[:])
-                nc.scalar.copy(out=x_words[:, pair * 2 * P : (pair + 1) * 2 * P, :], in_=xt[:].rearrange("p u w -> p w u"))
-            nc.vector.quantize_mx(
-                out=x_codes[:, g, :].bitcast(FP8X4),
-                scales=x_scales[:, g, :],
-                in_=x_grouped[:].rearrange("p w t -> p (w t)"),
-            )
+
+        def quantise_x():
+            for g in range(PASSES):
+                x_grouped = act_grouped_pool.tile(
+                    [P, TOKENS, PACK], BF16, name="x_grouped", tag="act_grouped", align_bytes=64
+                )
+                x_words = x_grouped[:].rearrange("p w t -> p (w t)").bitcast(F32).rearrange("p (w u) -> p w u", u=2)
+                for pair in range(TOKEN_TILES // 2):
+                    xt = psum.tile([P, 2, 2 * P], F32, name="xt", tag="bank")
+                    for s in range(2):
+                        words = x_sb[pair][:, s, :].bitcast(F32)
+                        for u in range(2):
+                            first = g * 2 * P + u * P
+                            nc.tensor.transpose(xt[:, u, s * P : (s + 1) * P], words[:, first : first + P], ident[:])
+                    nc.scalar.copy(
+                        out=x_words[:, pair * 2 * P : (pair + 1) * 2 * P, :], in_=xt[:].rearrange("p u w -> p w u")
+                    )
+                nc.vector.quantize_mx(
+                    out=x_codes[:, g, :].bitcast(FP8X4),
+                    scales=x_scales[:, g, :],
+                    in_=x_grouped[:].rearrange("p w t -> p (w t)"),
+                )
 
         weight_codes = {}
         weight_scales = {}
 
         def prepare_chunk(n):
             raw = raw_chunks[n]
-            grouped = grouped_pool.tile([P, CHUNK_COLS, PACK], BF16, name="grouped", tag="grouped", align_bytes=64)
-            dst = grouped[:].rearrange("p (c i) t -> p c t i", i=RUN)
             src = raw[:].rearrange("p t (c i) -> p c t i", i=RUN)
-            split = VECTOR_COLS // RUN
-            nc.vector.tensor_copy(out=dst[:, :split], in_=src[:, :split])
-            nc.scalar.copy(out=dst[:, split:], in_=src[:, split:])
             codes = weight_codes_pool.tile([P, CHUNK_COLS], U32, name="codes", tag="codes", align_bytes=64)
             scales = weight_codes_pool.tile([P, CHUNK_COLS], U8, name="scales", tag="scales", align_bytes=64)
+            split = VECTOR_COLS // RUN
+            left = grouped_pool.tile([P, VECTOR_COLS, PACK], BF16, name="left", tag="left", align_bytes=64)
+            right = grouped_pool.tile([P, CHUNK_COLS - VECTOR_COLS, PACK], BF16, name="right", tag="right", align_bytes=64)
+            nc.vector.tensor_copy(out=left[:].rearrange("p (c i) t -> p c t i", i=RUN), in_=src[:, :split])
+            nc.scalar.copy(out=right[:].rearrange("p (c i) t -> p c t i", i=RUN), in_=src[:, split:])
             nc.vector.quantize_mx(
-                out=codes[:].bitcast(FP8X4), scales=scales[:], in_=grouped[:].rearrange("p w t -> p (w t)")
+                out=codes[:, :VECTOR_COLS].bitcast(FP8X4),
+                scales=scales[:, :VECTOR_COLS],
+                in_=left[:].rearrange("p w t -> p (w t)"),
+            )
+            nc.vector.quantize_mx(
+                out=codes[:, VECTOR_COLS:].bitcast(FP8X4),
+                scales=scales[:, VECTOR_COLS:],
+                in_=right[:].rearrange("p w t -> p (w t)"),
             )
             weight_codes[n] = codes
             weight_scales[n] = scales
@@ -159,7 +178,7 @@ def tile_multiscaleretention_pc_kernel(tc, x, y_ret, w_g, w_proj, gn_weight, gn_
         normed = {}
 
         def normalise(group):
-            yn = gate_pool.tile([P, PACK, TOKENS], F32, name="yn", tag="yn")
+            yn = yn_pool.tile([P, PACK, TOKENS], F32, name="yn", tag="yn")
             for j in range(PACK):
                 h = group * PACK + j
                 z = z_pool.tile([P, TOKEN_TILES, HEAD_DIM], F32, name="z", tag="z")
@@ -188,68 +207,85 @@ def tile_multiscaleretention_pc_kernel(tc, x, y_ret, w_g, w_proj, gn_weight, gn_
         h_codes = const.tile([P, PASSES, TOKENS], U32, align_bytes=64)
         h_scales = const.tile([P, PASSES, TOKENS], U8, align_bytes=64)
 
-        def gate(group):
-            silu = gate_pool.tile([P, PACK, TOKENS], F32, name="silu", tag="silu")
-            for j in range(PACK):
-                c_tile = group * PACK + j
-                half = c_tile * P // CHUNK_COLS
-                cols = slice(c_tile * P - half * CHUNK_COLS, (c_tile + 1) * P - half * CHUNK_COLS)
-                acc = psum.tile([P, BANK], F32, name="acc", tag="bank")
-                for g in range(PASSES):
-                    n = half * PASSES + g
-                    nc.tensor.matmul_mx(
-                        out=acc[:],
-                        lhsT=weight_codes[n][:, cols].bitcast(FP8X4),
-                        lhsT_scale=weight_scales[n][:, cols],
-                        rhs=x_codes[:, g, :].bitcast(FP8X4),
-                        rhs_scale=x_scales[:, g, :],
-                        start=(g == 0),
-                        stop=(g == PASSES - 1),
-                    )
-                nc.scalar.activation(out=silu[:, j, :], in_=acc[:], func=ACT.Silu)
-            h_grouped = act_grouped_pool.tile([P, TOKENS, PACK], BF16, name="h_grouped", tag="act_grouped", align_bytes=64)
-            nc.vector.tensor_tensor(
-                out=h_grouped[:].rearrange("p (c i) t -> p c t i", i=RUN),
-                in0=silu[:].rearrange("p t (c i) -> p c t i", i=RUN),
-                in1=normed[group][:].rearrange("p t (c i) -> p c t i", i=RUN),
-                op=ALU.mult,
-            )
-            nc.vector.quantize_mx(
-                out=h_codes[:, group, :].bitcast(FP8X4),
-                scales=h_scales[:, group, :],
-                in_=h_grouped[:].rearrange("p w t -> p (w t)"),
-            )
+        gate_banks = {}
 
-        def project(m):
-            half = m * BANK // CHUNK_COLS
-            cols = slice(m * BANK - half * CHUNK_COLS, (m + 1) * BANK - half * CHUNK_COLS)
+        def gate_pass(n):
+            g = n % PASSES
+            for b in range(CHUNK_COLS // P):
+                if g == 0:
+                    gate_banks[b] = psum.tile([P, BANK], F32, name="gate_bank", tag="bank")
+                nc.tensor.matmul_mx(
+                    out=gate_banks[b][:],
+                    lhsT=weight_codes[n][:, b * P : (b + 1) * P].bitcast(FP8X4),
+                    lhsT_scale=weight_scales[n][:, b * P : (b + 1) * P],
+                    rhs=x_codes[:, g, :].bitcast(FP8X4),
+                    rhs_scale=x_scales[:, g, :],
+                    start=(g == 0),
+                    stop=(g == PASSES - 1),
+                )
+
+        def finish_gate(half):
+            for group in range(2 * half, 2 * half + 2):
+                silu = silu_pool.tile([P, PACK, TOKENS], F32, name="silu", tag="silu")
+                for j in range(PACK):
+                    nc.scalar.activation(out=silu[:, j, :], in_=gate_banks[(group % 2) * PACK + j][:], func=ACT.Silu)
+                h_grouped = act_grouped_pool.tile(
+                    [P, TOKENS, PACK], BF16, name="h_grouped", tag="act_grouped", align_bytes=64
+                )
+                nc.vector.tensor_tensor(
+                    out=h_grouped[:].rearrange("p (c i) t -> p c t i", i=RUN),
+                    in0=silu[:].rearrange("p t (c i) -> p c t i", i=RUN),
+                    in1=normed[group][:].rearrange("p t (c i) -> p c t i", i=RUN),
+                    op=ALU.mult,
+                )
+                nc.vector.quantize_mx(
+                    out=h_codes[:, group, :].bitcast(FP8X4),
+                    scales=h_scales[:, group, :],
+                    in_=h_grouped[:].rearrange("p w t -> p (w t)"),
+                )
+
+        out_banks = {}
+
+        def project(n):
+            half, group = (n - 8) // PASSES, n % PASSES
             for tt in range(TOKEN_TILES):
-                acc = psum.tile([P, BANK], F32, name="acc2", tag="bank")
-                for group in range(PASSES):
-                    n = 8 + half * PASSES + group
+                for b in range(CHUNK_COLS // BANK):
+                    if group == 0:
+                        out_banks[(tt, b)] = psum.tile([P, BANK], F32, name="out_bank", tag="bank")
                     nc.tensor.matmul_mx(
-                        out=acc[:],
+                        out=out_banks[(tt, b)][:],
                         lhsT=h_codes[:, group, tt * P : (tt + 1) * P].bitcast(FP8X4),
                         lhsT_scale=h_scales[:, group, tt * P : (tt + 1) * P],
-                        rhs=weight_codes[n][:, cols].bitcast(FP8X4),
-                        rhs_scale=weight_scales[n][:, cols],
+                        rhs=weight_codes[n][:, b * BANK : (b + 1) * BANK].bitcast(FP8X4),
+                        rhs_scale=weight_scales[n][:, b * BANK : (b + 1) * BANK],
                         start=(group == 0),
                         stop=(group == PASSES - 1),
                     )
-                stage = out_pool.tile([P, BANK], F32, name="stage", tag="stage")
-                nc.scalar.copy(out=stage[:], in_=acc[:])
-                nc.sync.dma_start(out=out_rows[tt * P : (tt + 1) * P, m * BANK : (m + 1) * BANK], in_=stage[:])
+            if group < PASSES - 1:
+                return
+            for tt in range(TOKEN_TILES):
+                for b in range(CHUNK_COLS // BANK):
+                    stage = out_pool.tile([P, BANK], F32, name="stage", tag="stage")
+                    if b == 1:
+                        nc.vector.tensor_copy(out=stage[:], in_=out_banks[(tt, b)][:])
+                    else:
+                        nc.scalar.copy(out=stage[:], in_=out_banks[(tt, b)][:])
+                    first = half * CHUNK_COLS + b * BANK
+                    nc.sync.dma_start(out=out_rows[tt * P : (tt + 1) * P, first : first + BANK], in_=stage[:])
 
+        for tt in range(TOKEN_TILES):
+            take_statistics(tt)
+        join_statistics()
+        quantise_x()
+        for group in range(PASSES):
+            normalise(group)
         for n in range(N_CHUNKS):
+            prepare_chunk(n)
             if n + PREFETCH < N_CHUNKS:
                 load_chunk(n + PREFETCH)
-            prepare_chunk(n)
-            if n % 2 == 1:
-                step = n // 2
-                if step < PASSES:
-                    normalise(step)
-                if 1 <= step <= PASSES:
-                    gate(step - 1)
-                if step > PASSES:
-                    project(step - PASSES - 1)
-        project(PASSES - 1)
+            if n < 8:
+                gate_pass(n)
+                if n % PASSES == PASSES - 1:
+                    finish_gate(n // PASSES)
+            else:
+                project(n)

@@ -27,7 +27,7 @@ HALVES = WIDTH // CHUNK_COLS
 N_CHUNKS = 2 * HALVES * PASSES
 PREFETCH = 3
 RUN = 4
-VECTOR_COLS = 512
+VECTOR_COLS = 640
 
 FLOPS = 2 * 2 * TOKENS * WIDTH * WIDTH
 
@@ -43,11 +43,10 @@ def tile_multiscaleretention_pc_kernel(tc, x, y_ret, w_g, w_proj, gn_weight, gn_
         raw_pool = ctx.enter_context(tc.tile_pool(name="raw", bufs=5))
         grouped_pool = ctx.enter_context(tc.tile_pool(name="grouped", bufs=3))
         act_grouped_pool = ctx.enter_context(tc.tile_pool(name="act_grouped", bufs=2))
-        weight_codes_pool = ctx.enter_context(tc.tile_pool(name="weight_codes", bufs=10))
+        weight_codes_pool = ctx.enter_context(tc.tile_pool(name="weight_codes", bufs=12))
         z_pool = ctx.enter_context(tc.tile_pool(name="z", bufs=4))
-        yn_pool = ctx.enter_context(tc.tile_pool(name="yn", bufs=4))
-        silu_pool = ctx.enter_context(tc.tile_pool(name="silu", bufs=2))
-        out_pool = ctx.enter_context(tc.tile_pool(name="out_stage", bufs=4))
+        gate_pool = ctx.enter_context(tc.tile_pool(name="gate", bufs=2))
+        out_pool = ctx.enter_context(tc.tile_pool(name="out_stage", bufs=6))
         psum = ctx.enter_context(tc.psum_pool(name="psum", bufs=8))
 
         raw_chunks = {}
@@ -98,11 +97,9 @@ def tile_multiscaleretention_pc_kernel(tc, x, y_ret, w_g, w_proj, gn_weight, gn_
 
         groups = TOKEN_TILES * HEADS
         stats = const.tile([P, groups, 6], F32)
-
-        def take_statistics(tt):
+        for tt in range(TOKEN_TILES):
             for h in range(HEADS):
                 nc.vector.bn_stats(out=stats[:, tt * HEADS + h, :], in_=y_sb[:, tt, h * HEAD_DIM : (h + 1) * HEAD_DIM])
-
         mean_even, m2_even = stats[:, :, 1], stats[:, :, 2]
         mean_odd, m2_odd = stats[:, :, 4], stats[:, :, 5]
         mean = const.tile([P, groups], F32)
@@ -110,67 +107,50 @@ def tile_multiscaleretention_pc_kernel(tc, x, y_ret, w_g, w_proj, gn_weight, gn_
         var = const.tile([P, groups], F32)
         std = const.tile([P, groups], F32)
         rstd = const.tile([P, groups], F32)
-
-        def join_statistics():
-            nc.vector.tensor_tensor(out=mean[:], in0=mean_even, in1=mean_odd, op=ALU.add)
-            nc.vector.tensor_scalar_mul(out=mean[:], in0=mean[:], scalar1=0.5)
-            nc.vector.tensor_tensor(out=gap[:], in0=mean_even, in1=mean_odd, op=ALU.subtract)
-            nc.vector.tensor_tensor(out=gap[:], in0=gap[:], in1=gap[:], op=ALU.mult)
-            nc.vector.tensor_tensor(out=var[:], in0=m2_even, in1=m2_odd, op=ALU.add)
-            nc.vector.tensor_scalar(
-                out=var[:], in0=var[:], scalar1=1.0 / HEAD_DIM, scalar2=EPS, op0=ALU.mult, op1=ALU.add
-            )
-            nc.vector.scalar_tensor_tensor(out=var[:], in0=gap[:], scalar=0.25, in1=var[:], op0=ALU.mult, op1=ALU.add)
-            nc.scalar.activation(out=std[:], in_=var[:], func=ACT.Sqrt)
-            nc.vector.reciprocal(out=rstd[:], in_=std[:])
+        nc.vector.tensor_tensor(out=mean[:], in0=mean_even, in1=mean_odd, op=ALU.add)
+        nc.vector.tensor_scalar_mul(out=mean[:], in0=mean[:], scalar1=0.5)
+        nc.vector.tensor_tensor(out=gap[:], in0=mean_even, in1=mean_odd, op=ALU.subtract)
+        nc.vector.tensor_tensor(out=gap[:], in0=gap[:], in1=gap[:], op=ALU.mult)
+        nc.vector.tensor_tensor(out=var[:], in0=m2_even, in1=m2_odd, op=ALU.add)
+        nc.vector.tensor_scalar(out=var[:], in0=var[:], scalar1=1.0 / HEAD_DIM, scalar2=EPS, op0=ALU.mult, op1=ALU.add)
+        nc.vector.scalar_tensor_tensor(out=var[:], in0=gap[:], scalar=0.25, in1=var[:], op0=ALU.mult, op1=ALU.add)
+        nc.scalar.activation(out=std[:], in_=var[:], func=ACT.Sqrt)
+        nc.vector.reciprocal(out=rstd[:], in_=std[:])
 
         x_codes = const.tile([P, PASSES, TOKENS], U32, align_bytes=64)
         x_scales = const.tile([P, PASSES, TOKENS], U8, align_bytes=64)
-
-        def quantise_x():
-            for g in range(PASSES):
-                x_grouped = act_grouped_pool.tile(
-                    [P, TOKENS, PACK], BF16, name="x_grouped", tag="act_grouped", align_bytes=64
-                )
-                x_words = x_grouped[:].rearrange("p w t -> p (w t)").bitcast(F32).rearrange("p (w u) -> p w u", u=2)
-                for pair in range(TOKEN_TILES // 2):
-                    xt = psum.tile([P, 2, 2 * P], F32, name="xt", tag="bank")
-                    for s in range(2):
-                        words = x_sb[pair][:, s, :].bitcast(F32)
-                        for u in range(2):
-                            first = g * 2 * P + u * P
-                            nc.tensor.transpose(xt[:, u, s * P : (s + 1) * P], words[:, first : first + P], ident[:])
-                    nc.scalar.copy(
-                        out=x_words[:, pair * 2 * P : (pair + 1) * 2 * P, :], in_=xt[:].rearrange("p u w -> p w u")
-                    )
-                nc.vector.quantize_mx(
-                    out=x_codes[:, g, :].bitcast(FP8X4),
-                    scales=x_scales[:, g, :],
-                    in_=x_grouped[:].rearrange("p w t -> p (w t)"),
-                )
+        for g in range(PASSES):
+            x_grouped = act_grouped_pool.tile([P, TOKENS, PACK], BF16, name="x_grouped", tag="act_grouped", align_bytes=64)
+            x_words = x_grouped[:].rearrange("p w t -> p (w t)").bitcast(F32).rearrange("p (w u) -> p w u", u=2)
+            for pair in range(TOKEN_TILES // 2):
+                xt = psum.tile([P, 2, 2 * P], F32, name="xt", tag="bank")
+                for s in range(2):
+                    words = x_sb[pair][:, s, :].bitcast(F32)
+                    for u in range(2):
+                        first = g * 2 * P + u * P
+                        nc.tensor.transpose(xt[:, u, s * P : (s + 1) * P], words[:, first : first + P], ident[:])
+                nc.scalar.copy(out=x_words[:, pair * 2 * P : (pair + 1) * 2 * P, :], in_=xt[:].rearrange("p u w -> p w u"))
+            nc.vector.quantize_mx(
+                out=x_codes[:, g, :].bitcast(FP8X4),
+                scales=x_scales[:, g, :],
+                in_=x_grouped[:].rearrange("p w t -> p (w t)"),
+            )
 
         weight_codes = {}
         weight_scales = {}
 
         def prepare_chunk(n):
             raw = raw_chunks[n]
+            grouped = grouped_pool.tile([P, CHUNK_COLS, PACK], BF16, name="grouped", tag="grouped", align_bytes=64)
+            dst = grouped[:].rearrange("p (c i) t -> p c t i", i=RUN)
             src = raw[:].rearrange("p t (c i) -> p c t i", i=RUN)
+            split = VECTOR_COLS // RUN
+            nc.vector.tensor_copy(out=dst[:, :split], in_=src[:, :split])
+            nc.scalar.copy(out=dst[:, split:], in_=src[:, split:])
             codes = weight_codes_pool.tile([P, CHUNK_COLS], U32, name="codes", tag="codes", align_bytes=64)
             scales = weight_codes_pool.tile([P, CHUNK_COLS], U8, name="scales", tag="scales", align_bytes=64)
-            split = VECTOR_COLS // RUN
-            left = grouped_pool.tile([P, VECTOR_COLS, PACK], BF16, name="left", tag="left", align_bytes=64)
-            right = grouped_pool.tile([P, CHUNK_COLS - VECTOR_COLS, PACK], BF16, name="right", tag="right", align_bytes=64)
-            nc.vector.tensor_copy(out=left[:].rearrange("p (c i) t -> p c t i", i=RUN), in_=src[:, :split])
-            nc.scalar.copy(out=right[:].rearrange("p (c i) t -> p c t i", i=RUN), in_=src[:, split:])
             nc.vector.quantize_mx(
-                out=codes[:, :VECTOR_COLS].bitcast(FP8X4),
-                scales=scales[:, :VECTOR_COLS],
-                in_=left[:].rearrange("p w t -> p (w t)"),
-            )
-            nc.vector.quantize_mx(
-                out=codes[:, VECTOR_COLS:].bitcast(FP8X4),
-                scales=scales[:, VECTOR_COLS:],
-                in_=right[:].rearrange("p w t -> p (w t)"),
+                out=codes[:].bitcast(FP8X4), scales=scales[:], in_=grouped[:].rearrange("p w t -> p (w t)")
             )
             weight_codes[n] = codes
             weight_scales[n] = scales
@@ -178,7 +158,7 @@ def tile_multiscaleretention_pc_kernel(tc, x, y_ret, w_g, w_proj, gn_weight, gn_
         normed = {}
 
         def normalise(group):
-            yn = yn_pool.tile([P, PACK, TOKENS], F32, name="yn", tag="yn")
+            yn = gate_pool.tile([P, PACK, TOKENS], F32, name="yn", tag="yn")
             for j in range(PACK):
                 h = group * PACK + j
                 z = z_pool.tile([P, TOKEN_TILES, HEAD_DIM], F32, name="z", tag="z")
@@ -207,42 +187,37 @@ def tile_multiscaleretention_pc_kernel(tc, x, y_ret, w_g, w_proj, gn_weight, gn_
         h_codes = const.tile([P, PASSES, TOKENS], U32, align_bytes=64)
         h_scales = const.tile([P, PASSES, TOKENS], U8, align_bytes=64)
 
-        gate_banks = {}
-
-        def gate_pass(n):
-            g = n % PASSES
-            for b in range(CHUNK_COLS // P):
-                if g == 0:
-                    gate_banks[b] = psum.tile([P, BANK], F32, name="gate_bank", tag="bank")
-                nc.tensor.matmul_mx(
-                    out=gate_banks[b][:],
-                    lhsT=weight_codes[n][:, b * P : (b + 1) * P].bitcast(FP8X4),
-                    lhsT_scale=weight_scales[n][:, b * P : (b + 1) * P],
-                    rhs=x_codes[:, g, :].bitcast(FP8X4),
-                    rhs_scale=x_scales[:, g, :],
-                    start=(g == 0),
-                    stop=(g == PASSES - 1),
-                )
-
-        def finish_gate(half):
-            for group in range(2 * half, 2 * half + 2):
-                silu = silu_pool.tile([P, PACK, TOKENS], F32, name="silu", tag="silu")
-                for j in range(PACK):
-                    nc.scalar.activation(out=silu[:, j, :], in_=gate_banks[(group % 2) * PACK + j][:], func=ACT.Silu)
-                h_grouped = act_grouped_pool.tile(
-                    [P, TOKENS, PACK], BF16, name="h_grouped", tag="act_grouped", align_bytes=64
-                )
-                nc.vector.tensor_tensor(
-                    out=h_grouped[:].rearrange("p (c i) t -> p c t i", i=RUN),
-                    in0=silu[:].rearrange("p t (c i) -> p c t i", i=RUN),
-                    in1=normed[group][:].rearrange("p t (c i) -> p c t i", i=RUN),
-                    op=ALU.mult,
-                )
-                nc.vector.quantize_mx(
-                    out=h_codes[:, group, :].bitcast(FP8X4),
-                    scales=h_scales[:, group, :],
-                    in_=h_grouped[:].rearrange("p w t -> p (w t)"),
-                )
+        def gate(group):
+            silu = gate_pool.tile([P, PACK, TOKENS], F32, name="silu", tag="silu")
+            for j in range(PACK):
+                c_tile = group * PACK + j
+                half = c_tile * P // CHUNK_COLS
+                cols = slice(c_tile * P - half * CHUNK_COLS, (c_tile + 1) * P - half * CHUNK_COLS)
+                acc = psum.tile([P, BANK], F32, name="acc", tag="bank")
+                for g in range(PASSES):
+                    n = half * PASSES + g
+                    nc.tensor.matmul_mx(
+                        out=acc[:],
+                        lhsT=weight_codes[n][:, cols].bitcast(FP8X4),
+                        lhsT_scale=weight_scales[n][:, cols],
+                        rhs=x_codes[:, g, :].bitcast(FP8X4),
+                        rhs_scale=x_scales[:, g, :],
+                        start=(g == 0),
+                        stop=(g == PASSES - 1),
+                    )
+                nc.scalar.activation(out=silu[:, j, :], in_=acc[:], func=ACT.Silu)
+            h_grouped = act_grouped_pool.tile([P, TOKENS, PACK], BF16, name="h_grouped", tag="act_grouped", align_bytes=64)
+            nc.vector.tensor_tensor(
+                out=h_grouped[:].rearrange("p (c i) t -> p c t i", i=RUN),
+                in0=silu[:].rearrange("p t (c i) -> p c t i", i=RUN),
+                in1=normed[group][:].rearrange("p t (c i) -> p c t i", i=RUN),
+                op=ALU.mult,
+            )
+            nc.vector.quantize_mx(
+                out=h_codes[:, group, :].bitcast(FP8X4),
+                scales=h_scales[:, group, :],
+                in_=h_grouped[:].rearrange("p w t -> p (w t)"),
+            )
 
         out_banks = {}
 
@@ -266,26 +241,27 @@ def tile_multiscaleretention_pc_kernel(tc, x, y_ret, w_g, w_proj, gn_weight, gn_
             for tt in range(TOKEN_TILES):
                 for b in range(CHUNK_COLS // BANK):
                     stage = out_pool.tile([P, BANK], F32, name="stage", tag="stage")
-                    if b == 1:
+                    if half == HALVES - 1 and b == 1:
                         nc.vector.tensor_copy(out=stage[:], in_=out_banks[(tt, b)][:])
                     else:
                         nc.scalar.copy(out=stage[:], in_=out_banks[(tt, b)][:])
                     first = half * CHUNK_COLS + b * BANK
                     nc.sync.dma_start(out=out_rows[tt * P : (tt + 1) * P, first : first + BANK], in_=stage[:])
 
-        for tt in range(TOKEN_TILES):
-            take_statistics(tt)
-        join_statistics()
-        quantise_x()
-        for group in range(PASSES):
-            normalise(group)
+        waiting = []
         for n in range(N_CHUNKS):
             prepare_chunk(n)
             if n + PREFETCH < N_CHUNKS:
                 load_chunk(n + PREFETCH)
-            if n < 8:
-                gate_pass(n)
-                if n % PASSES == PASSES - 1:
-                    finish_gate(n // PASSES)
-            else:
-                project(n)
+            step = n // 2
+            if n % 2 == 1:
+                if step < PASSES:
+                    normalise(step)
+                if 1 <= step <= PASSES:
+                    gate(step - 1)
+            if n >= 8:
+                waiting.append(n)
+            if n > 2 * PASSES:
+                for ready in waiting:
+                    project(ready)
+                waiting = []

@@ -28,6 +28,7 @@ N_CHUNKS = 2 * HALVES * PASSES
 PREFETCH = 3
 RUN = 4
 VECTOR_COLS = 640
+GPSIMD_CHUNKS = 3
 
 FLOPS = 2 * 2 * TOKENS * WIDTH * WIDTH
 
@@ -145,7 +146,17 @@ def tile_multiscaleretention_pc_kernel(tc, x, y_ret, w_g, w_proj, gn_weight, gn_
             dst = grouped[:].rearrange("p (c i) t -> p c t i", i=RUN)
             src = raw[:].rearrange("p t (c i) -> p c t i", i=RUN)
             split = VECTOR_COLS // RUN
-            nc.vector.tensor_copy(out=dst[:, :split], in_=src[:, :split])
+            if n < GPSIMD_CHUNKS:
+                nc.gpsimd.tensor_scalar(
+                    out=grouped[:, :VECTOR_COLS, :],
+                    in0=raw[:, :, :VECTOR_COLS].rearrange("p t c -> p c t"),
+                    scalar1=1.0,
+                    scalar2=0.0,
+                    op0=ALU.mult,
+                    op1=ALU.add,
+                )
+            else:
+                nc.vector.tensor_copy(out=dst[:, :split], in_=src[:, :split])
             nc.scalar.copy(out=dst[:, split:], in_=src[:, split:])
             codes = weight_codes_pool.tile([P, CHUNK_COLS], U32, name="codes", tag="codes", align_bytes=64)
             scales = weight_codes_pool.tile([P, CHUNK_COLS], U8, name="scales", tag="scales", align_bytes=64)

@@ -29,6 +29,7 @@ PREFETCH = 3
 RUN = 4
 VECTOR_COLS = 640
 GPSIMD_CHUNKS = 3
+GPSIMD_COLS = 384
 
 FLOPS = 2 * 2 * TOKENS * WIDTH * WIDTH
 
@@ -47,7 +48,7 @@ def tile_multiscaleretention_pc_kernel(tc, x, y_ret, w_g, w_proj, gn_weight, gn_
         weight_codes_pool = ctx.enter_context(tc.tile_pool(name="weight_codes", bufs=12))
         z_pool = ctx.enter_context(tc.tile_pool(name="z", bufs=4))
         gate_pool = ctx.enter_context(tc.tile_pool(name="gate", bufs=2))
-        out_pool = ctx.enter_context(tc.tile_pool(name="out_stage", bufs=6))
+        out_pool = ctx.enter_context(tc.tile_pool(name="out_stage", bufs=8))
         psum = ctx.enter_context(tc.psum_pool(name="psum", bufs=8))
 
         raw_chunks = {}
@@ -97,24 +98,19 @@ def tile_multiscaleretention_pc_kernel(tc, x, y_ret, w_g, w_proj, gn_weight, gn_
         nc.vector.tensor_copy(out=gain_cols[:], in_=gain_bank[:, 0 : 2 * HEADS])
 
         groups = TOKEN_TILES * HEADS
-        stats = const.tile([P, groups, 6], F32)
+        stats = const.tile([P, groups // 2, 6], F32)
         for tt in range(TOKEN_TILES):
-            for h in range(HEADS):
-                nc.vector.bn_stats(out=stats[:, tt * HEADS + h, :], in_=y_sb[:, tt, h * HEAD_DIM : (h + 1) * HEAD_DIM])
-        mean_even, m2_even = stats[:, :, 1], stats[:, :, 2]
-        mean_odd, m2_odd = stats[:, :, 4], stats[:, :, 5]
-        mean = const.tile([P, groups], F32)
-        gap = const.tile([P, groups], F32)
+            for pair in range(HEADS // 2):
+                nc.vector.bn_stats(
+                    out=stats[:, tt * HEADS // 2 + pair, :],
+                    in_=y_sb[:, tt, 2 * pair * HEAD_DIM : 2 * (pair + 1) * HEAD_DIM].rearrange("p (h c) -> p c h", h=2),
+                )
+        moments = stats[:].rearrange("p g (h s) -> p (g h) s", h=2)
+        mean = moments[:, :, 1]
         var = const.tile([P, groups], F32)
         std = const.tile([P, groups], F32)
         rstd = const.tile([P, groups], F32)
-        nc.vector.tensor_tensor(out=mean[:], in0=mean_even, in1=mean_odd, op=ALU.add)
-        nc.vector.tensor_scalar_mul(out=mean[:], in0=mean[:], scalar1=0.5)
-        nc.vector.tensor_tensor(out=gap[:], in0=mean_even, in1=mean_odd, op=ALU.subtract)
-        nc.vector.tensor_tensor(out=gap[:], in0=gap[:], in1=gap[:], op=ALU.mult)
-        nc.vector.tensor_tensor(out=var[:], in0=m2_even, in1=m2_odd, op=ALU.add)
-        nc.vector.tensor_scalar(out=var[:], in0=var[:], scalar1=1.0 / HEAD_DIM, scalar2=EPS, op0=ALU.mult, op1=ALU.add)
-        nc.vector.scalar_tensor_tensor(out=var[:], in0=gap[:], scalar=0.25, in1=var[:], op0=ALU.mult, op1=ALU.add)
+        nc.vector.tensor_scalar(out=var[:], in0=moments[:, :, 2], scalar1=1.0 / HEAD_DIM, scalar2=EPS, op0=ALU.mult, op1=ALU.add)
         nc.scalar.activation(out=std[:], in_=var[:], func=ACT.Sqrt)
         nc.vector.reciprocal(out=rstd[:], in_=std[:])
 
@@ -145,26 +141,37 @@ def tile_multiscaleretention_pc_kernel(tc, x, y_ret, w_g, w_proj, gn_weight, gn_
             grouped = grouped_pool.tile([P, CHUNK_COLS, PACK], BF16, name="grouped", tag="grouped", align_bytes=64)
             dst = grouped[:].rearrange("p (c i) t -> p c t i", i=RUN)
             src = raw[:].rearrange("p t (c i) -> p c t i", i=RUN)
-            split = VECTOR_COLS // RUN
+            first_cols = GPSIMD_COLS if n < GPSIMD_CHUNKS else VECTOR_COLS
+            split = first_cols // RUN
             if n < GPSIMD_CHUNKS:
                 nc.gpsimd.tensor_scalar(
-                    out=grouped[:, :VECTOR_COLS, :],
-                    in0=raw[:, :, :VECTOR_COLS].rearrange("p t c -> p c t"),
+                    out=grouped[:, :first_cols, :],
+                    in0=raw[:, :, :first_cols].rearrange("p t c -> p c t"),
                     scalar1=1.0,
                     scalar2=0.0,
                     op0=ALU.mult,
                     op1=ALU.add,
                 )
-            else:
+            elif n < N_CHUNKS - 1:
                 nc.vector.tensor_copy(out=dst[:, :split], in_=src[:, :split])
-            nc.scalar.copy(out=dst[:, split:], in_=src[:, split:])
             codes = weight_codes_pool.tile([P, CHUNK_COLS], U32, name="codes", tag="codes", align_bytes=64)
             scales = weight_codes_pool.tile([P, CHUNK_COLS], U8, name="scales", tag="scales", align_bytes=64)
-            nc.vector.quantize_mx(
-                out=codes[:].bitcast(FP8X4), scales=scales[:], in_=grouped[:].rearrange("p w t -> p (w t)")
-            )
             weight_codes[n] = codes
             weight_scales[n] = scales
+            flat = grouped[:].rearrange("p w t -> p (w t)")
+            if n < N_CHUNKS - 1:
+                nc.scalar.copy(out=dst[:, split:], in_=src[:, split:])
+                nc.vector.quantize_mx(out=codes[:].bitcast(FP8X4), scales=scales[:], in_=flat)
+                return
+            runs = BANK // RUN
+            for b in range(CHUNK_COLS // BANK):
+                nc.vector.tensor_copy(out=dst[:, b * runs : b * runs + split // 2], in_=src[:, b * runs : b * runs + split // 2])
+                nc.scalar.copy(out=dst[:, b * runs + split // 2 : (b + 1) * runs], in_=src[:, b * runs + split // 2 : (b + 1) * runs])
+                nc.vector.quantize_mx(
+                    out=codes[:, b * BANK : (b + 1) * BANK].bitcast(FP8X4),
+                    scales=scales[:, b * BANK : (b + 1) * BANK],
+                    in_=flat[:, b * BANK * PACK : (b + 1) * BANK * PACK],
+                )
 
         normed = {}
 
@@ -234,8 +241,8 @@ def tile_multiscaleretention_pc_kernel(tc, x, y_ret, w_g, w_proj, gn_weight, gn_
 
         def project(n):
             half, group = (n - 8) // PASSES, n % PASSES
-            for tt in range(TOKEN_TILES):
-                for b in range(CHUNK_COLS // BANK):
+            for b in range(CHUNK_COLS // BANK):
+                for tt in range(TOKEN_TILES):
                     if group == 0:
                         out_banks[(tt, b)] = psum.tile([P, BANK], F32, name="out_bank", tag="bank")
                     nc.tensor.matmul_mx(
@@ -249,10 +256,10 @@ def tile_multiscaleretention_pc_kernel(tc, x, y_ret, w_g, w_proj, gn_weight, gn_
                     )
             if group < PASSES - 1:
                 return
-            for tt in range(TOKEN_TILES):
-                for b in range(CHUNK_COLS // BANK):
+            for b in range(CHUNK_COLS // BANK):
+                for tt in range(TOKEN_TILES):
                     stage = out_pool.tile([P, BANK], F32, name="stage", tag="stage")
-                    if half == HALVES - 1 and b == 1:
+                    if half == HALVES - 1 and tt % 2 == 1:
                         nc.vector.tensor_copy(out=stage[:], in_=out_banks[(tt, b)][:])
                     else:
                         nc.scalar.copy(out=stage[:], in_=out_banks[(tt, b)][:])

@@ -26,7 +26,8 @@ CHUNK_COLS = 1024
 HALVES = WIDTH // CHUNK_COLS
 N_CHUNKS = 2 * HALVES * PASSES
 PREFETCH = 3
-RUN = 4
+RUN = 8
+GATE_RUN = 4
 VECTOR_COLS = 640
 GPSIMD_CHUNKS = 3
 GPSIMD_COLS = 384
@@ -226,9 +227,9 @@ def tile_multiscaleretention_pc_kernel(tc, x, y_ret, w_g, w_proj, gn_weight, gn_
                 nc.scalar.activation(out=silu[:, j, :], in_=acc[:], func=ACT.Silu)
             h_grouped = act_grouped_pool.tile([P, TOKENS, PACK], BF16, name="h_grouped", tag="act_grouped", align_bytes=64)
             nc.vector.tensor_tensor(
-                out=h_grouped[:].rearrange("p (c i) t -> p c t i", i=RUN),
-                in0=silu[:].rearrange("p t (c i) -> p c t i", i=RUN),
-                in1=normed[group][:].rearrange("p t (c i) -> p c t i", i=RUN),
+                out=h_grouped[:].rearrange("p (c i) t -> p c t i", i=GATE_RUN),
+                in0=silu[:].rearrange("p t (c i) -> p c t i", i=GATE_RUN),
+                in1=normed[group][:].rearrange("p t (c i) -> p c t i", i=GATE_RUN),
                 op=ALU.mult,
             )
             nc.vector.quantize_mx(

@@ -206,6 +206,8 @@ def tile_multiscaleretention_pc_kernel(tc, x, y_ret, w_g, w_proj, gn_weight, gn_
         h_codes = const.tile([P, PASSES, TOKENS], U32, align_bytes=64)
         h_scales = const.tile([P, PASSES, TOKENS], U8, align_bytes=64)
 
+        gated = {}
+
         def gate(group):
             silu = gate_pool.tile([P, PACK, TOKENS], F32, name="silu", tag="silu")
             for j in range(PACK):
@@ -232,10 +234,13 @@ def tile_multiscaleretention_pc_kernel(tc, x, y_ret, w_g, w_proj, gn_weight, gn_
                 in1=normed[group][:].rearrange("p t (c i) -> p c t i", i=GATE_RUN),
                 op=ALU.mult,
             )
+            gated[group] = h_grouped
+
+        def quantise_gate(group):
             nc.vector.quantize_mx(
                 out=h_codes[:, group, :].bitcast(FP8X4),
                 scales=h_scales[:, group, :],
-                in_=h_grouped[:].rearrange("p w t -> p (w t)"),
+                in_=gated[group][:].rearrange("p w t -> p (w t)"),
             )
 
         out_banks = {}
@@ -273,6 +278,8 @@ def tile_multiscaleretention_pc_kernel(tc, x, y_ret, w_g, w_proj, gn_weight, gn_
             if n + PREFETCH < N_CHUNKS:
                 load_chunk(n + PREFETCH)
             step = n // 2
+            if n % 2 == 0 and 2 <= step <= PASSES + 1:
+                quantise_gate(step - 2)
             if n % 2 == 1:
                 if step < PASSES:
                     normalise(step)

@@ -28,7 +28,7 @@ N_CHUNKS = 2 * HALVES * PASSES
 PREFETCH = 3
 RUN = 8
 GATE_RUN = 4
-VECTOR_COLS = 640
+VECTOR_COLS = 608
 GPSIMD_CHUNKS = 3
 GPSIMD_COLS = 384
 

from contextlib import ExitStack

import concourse.mybir as mybir
from concourse.masks import make_identity

F32 = mybir.dt.float32
BF16 = mybir.dt.bfloat16
U32 = mybir.dt.uint32
U8 = mybir.dt.uint8
FP8X4 = mybir.dt.float8_e4m3fn_x4
ACT = mybir.ActivationFunctionType
ALU = mybir.AluOpType

P = 128
PACK = 4
K_PASS = P * PACK
TOKENS = 512
WIDTH = 2048
HEADS = 16
HEAD_DIM = 128
EPS = 1e-5
PASSES = WIDTH // K_PASS
TOKEN_TILES = TOKENS // P
BANK = 512
CHUNK_COLS = 1024
HALVES = WIDTH // CHUNK_COLS
N_CHUNKS = 2 * HALVES * PASSES
PREFETCH = 3
RUN = 8
GATE_RUN = 4
VECTOR_COLS = 608
GPSIMD_CHUNKS = 3
GPSIMD_COLS = 384

FLOPS = 2 * 2 * TOKENS * WIDTH * WIDTH


def tile_multiscaleretention_pc_kernel(tc, x, y_ret, w_g, w_proj, gn_weight, gn_bias, out):
    nc = tc.nc
    x_rows = x.rearrange("b t e -> (b t) e")
    y_rows = y_ret.rearrange("b t c -> (b t) c")
    out_rows = out.rearrange("b t e -> (b t) e")

    with ExitStack() as ctx:
        const = ctx.enter_context(tc.tile_pool(name="const", bufs=1))
        raw_pool = ctx.enter_context(tc.tile_pool(name="raw", bufs=5))
        grouped_pool = ctx.enter_context(tc.tile_pool(name="grouped", bufs=3))
        act_grouped_pool = ctx.enter_context(tc.tile_pool(name="act_grouped", bufs=2))
        weight_codes_pool = ctx.enter_context(tc.tile_pool(name="weight_codes", bufs=12))
        z_pool = ctx.enter_context(tc.tile_pool(name="z", bufs=4))
        gate_pool = ctx.enter_context(tc.tile_pool(name="gate", bufs=2))
        out_pool = ctx.enter_context(tc.tile_pool(name="out_stage", bufs=8))
        psum = ctx.enter_context(tc.psum_pool(name="psum", bufs=8))

        raw_chunks = {}

        def load_chunk(n):
            raw = raw_pool.tile([P, PACK, CHUNK_COLS], BF16, name="raw", tag="raw")
            half, k_pass = (n % 8) // PASSES, n % PASSES
            rows = slice(k_pass * K_PASS, (k_pass + 1) * K_PASS)
            cols = slice(half * CHUNK_COLS, (half + 1) * CHUNK_COLS)
            if n < 8:
                for u in range(2):
                    part = slice(k_pass * K_PASS + u * 2 * P, k_pass * K_PASS + (u + 1) * 2 * P)
                    nc.sync.dma_start(
                        out=raw[:, 2 * u : 2 * u + 2, :],
                        in_=w_g[part, cols].rearrange("(q e) c -> q e c", e=2),
                    )
            else:
                nc.sync.dma_start(out=raw[:], in_=w_proj[rows, cols].rearrange("(j p) n -> p j n", p=P))
            raw_chunks[n] = raw

        y_sb = const.tile([P, TOKEN_TILES, WIDTH], BF16)
        for tt in range(TOKEN_TILES):
            nc.sync.dma_start(out=y_sb[:, tt, :], in_=y_rows[tt * P : (tt + 1) * P, :])
            if tt < PREFETCH:
                load_chunk(tt)
        x_sb = []
        for pair in range(TOKEN_TILES // 2):
            x_pair = raw_pool.tile([P, 2, WIDTH], BF16, name="x_pair", tag="raw")
            nc.sync.dma_start(
                out=x_pair[:],
                in_=x_rows[pair * 2 * P : (pair + 1) * 2 * P, :].rearrange("(s p) e -> p s e", p=P),
            )
            x_sb.append(x_pair)

        ident = const.tile([P, P], F32)
        make_identity(nc, ident[:])

        gain_rows = const.tile([P, P], BF16)
        nc.vector.memset(gain_rows[:], 0.0)
        nc.scalar.dma_start(out=gain_rows[0:HEADS, :], in_=gn_weight.rearrange("(h c) -> h c", c=HEAD_DIM))
        nc.scalar.dma_start(out=gain_rows[HEADS : 2 * HEADS, :], in_=gn_bias.rearrange("(h c) -> h c", c=HEAD_DIM))
        gain_rows_f32 = const.tile([P, P], F32)
        nc.vector.tensor_copy(out=gain_rows_f32[:], in_=gain_rows[:])
        gain_bank = psum.tile([P, BANK], F32, name="gain_bank", tag="bank")
        nc.tensor.transpose(gain_bank[:, 0:P], gain_rows_f32[:], ident[:])
        gain_cols = const.tile([P, 2 * HEADS], F32)
        nc.vector.tensor_copy(out=gain_cols[:], in_=gain_bank[:, 0 : 2 * HEADS])

        groups = TOKEN_TILES * HEADS
        stats = const.tile([P, groups // 2, 6], F32)
        for tt in range(TOKEN_TILES):
            for pair in range(HEADS // 2):
                nc.vector.bn_stats(
                    out=stats[:, tt * HEADS // 2 + pair, :],
                    in_=y_sb[:, tt, 2 * pair * HEAD_DIM : 2 * (pair + 1) * HEAD_DIM].rearrange("p (h c) -> p c h", h=2),
                )
        moments = stats[:].rearrange("p g (h s) -> p (g h) s", h=2)
        mean = moments[:, :, 1]
        var = const.tile([P, groups], F32)
        std = const.tile([P, groups], F32)
        rstd = const.tile([P, groups], F32)
        nc.vector.tensor_scalar(out=var[:], in0=moments[:, :, 2], scalar1=1.0 / HEAD_DIM, scalar2=EPS, op0=ALU.mult, op1=ALU.add)
        nc.scalar.activation(out=std[:], in_=var[:], func=ACT.Sqrt)
        nc.vector.reciprocal(out=rstd[:], in_=std[:])

        x_codes = const.tile([P, PASSES, TOKENS], U32, align_bytes=64)
        x_scales = const.tile([P, PASSES, TOKENS], U8, align_bytes=64)
        for g in range(PASSES):
            x_grouped = act_grouped_pool.tile([P, TOKENS, PACK], BF16, name="x_grouped", tag="act_grouped", align_bytes=64)
            x_words = x_grouped[:].rearrange("p w t -> p (w t)").bitcast(F32).rearrange("p (w u) -> p w u", u=2)
            for pair in range(TOKEN_TILES // 2):
                xt = psum.tile([P, 2, 2 * P], F32, name="xt", tag="bank")
                for s in range(2):
                    words = x_sb[pair][:, s, :].bitcast(F32)
                    for u in range(2):
                        first = g * 2 * P + u * P
                        nc.tensor.transpose(xt[:, u, s * P : (s + 1) * P], words[:, first : first + P], ident[:])
                nc.scalar.copy(out=x_words[:, pair * 2 * P : (pair + 1) * 2 * P, :], in_=xt[:].rearrange("p u w -> p w u"))
            nc.vector.quantize_mx(
                out=x_codes[:, g, :].bitcast(FP8X4),
                scales=x_scales[:, g, :],
                in_=x_grouped[:].rearrange("p w t -> p (w t)"),
            )

        weight_codes = {}
        weight_scales = {}

        def prepare_chunk(n):
            raw = raw_chunks[n]
            grouped = grouped_pool.tile([P, CHUNK_COLS, PACK], BF16, name="grouped", tag="grouped", align_bytes=64)
            dst = grouped[:].rearrange("p (c i) t -> p c t i", i=RUN)
            src = raw[:].rearrange("p t (c i) -> p c t i", i=RUN)
            first_cols = GPSIMD_COLS if n < GPSIMD_CHUNKS else VECTOR_COLS
            split = first_cols // RUN
            if n < GPSIMD_CHUNKS:
                nc.gpsimd.tensor_scalar(
                    out=grouped[:, :first_cols, :],
                    in0=raw[:, :, :first_cols].rearrange("p t c -> p c t"),
                    scalar1=1.0,
                    scalar2=0.0,
                    op0=ALU.mult,
                    op1=ALU.add,
                )
            elif n < N_CHUNKS - 1:
                nc.vector.tensor_copy(out=dst[:, :split], in_=src[:, :split])
            codes = weight_codes_pool.tile([P, CHUNK_COLS], U32, name="codes", tag="codes", align_bytes=64)
            scales = weight_codes_pool.tile([P, CHUNK_COLS], U8, name="scales", tag="scales", align_bytes=64)
            weight_codes[n] = codes
            weight_scales[n] = scales
            flat = grouped[:].rearrange("p w t -> p (w t)")
            if n < N_CHUNKS - 1:
                nc.scalar.copy(out=dst[:, split:], in_=src[:, split:])
                nc.vector.quantize_mx(out=codes[:].bitcast(FP8X4), scales=scales[:], in_=flat)
                return
            runs = BANK // RUN
            for b in range(CHUNK_COLS // BANK):
                nc.vector.tensor_copy(out=dst[:, b * runs : b * runs + split // 2], in_=src[:, b * runs : b * runs + split // 2])
                nc.scalar.copy(out=dst[:, b * runs + split // 2 : (b + 1) * runs], in_=src[:, b * runs + split // 2 : (b + 1) * runs])
                nc.vector.quantize_mx(
                    out=codes[:, b * BANK : (b + 1) * BANK].bitcast(FP8X4),
                    scales=scales[:, b * BANK : (b + 1) * BANK],
                    in_=flat[:, b * BANK * PACK : (b + 1) * BANK * PACK],
                )

        normed = {}

        def normalise(group):
            yn = gate_pool.tile([P, PACK, TOKENS], F32, name="yn", tag="yn")
            for j in range(PACK):
                h = group * PACK + j
                z = z_pool.tile([P, TOKEN_TILES, HEAD_DIM], F32, name="z", tag="z")
                for tt in range(TOKEN_TILES):
                    col = tt * HEADS + h
                    nc.vector.tensor_scalar(
                        out=z[:, tt, :],
                        in0=y_sb[:, tt, h * HEAD_DIM : (h + 1) * HEAD_DIM],
                        scalar1=mean[:, col : col + 1],
                        scalar2=rstd[:, col : col + 1],
                        op0=ALU.subtract,
                        op1=ALU.mult,
                    )
                zt = psum.tile([P, BANK], F32, name="zt", tag="bank")
                for tt in range(TOKEN_TILES):
                    nc.tensor.transpose(zt[:, tt * P : (tt + 1) * P], z[:, tt, :], ident[:])
                nc.scalar.activation(
                    out=yn[:, j, :],
                    in_=zt[:],
                    func=ACT.Identity,
                    scale=gain_cols[:, h : h + 1],
                    bias=gain_cols[:, HEADS + h : HEADS + h + 1],
                )
            normed[group] = yn

        h_codes = const.tile([P, PASSES, TOKENS], U32, align_bytes=64)
        h_scales = const.tile([P, PASSES, TOKENS], U8, align_bytes=64)

        gated = {}

        def gate(group):
            silu = gate_pool.tile([P, PACK, TOKENS], F32, name="silu", tag="silu")
            for j in range(PACK):
                c_tile = group * PACK + j
                half = c_tile * P // CHUNK_COLS
                cols = slice(c_tile * P - half * CHUNK_COLS, (c_tile + 1) * P - half * CHUNK_COLS)
                acc = psum.tile([P, BANK], F32, name="acc", tag="bank")
                for g in range(PASSES):
                    n = half * PASSES + g
                    nc.tensor.matmul_mx(
                        out=acc[:],
                        lhsT=weight_codes[n][:, cols].bitcast(FP8X4),
                        lhsT_scale=weight_scales[n][:, cols],
                        rhs=x_codes[:, g, :].bitcast(FP8X4),
                        rhs_scale=x_scales[:, g, :],
                        start=(g == 0),
                        stop=(g == PASSES - 1),
                    )
                nc.scalar.activation(out=silu[:, j, :], in_=acc[:], func=ACT.Silu)
            h_grouped = act_grouped_pool.tile([P, TOKENS, PACK], BF16, name="h_grouped", tag="act_grouped", align_bytes=64)
            nc.vector.tensor_tensor(
                out=h_grouped[:].rearrange("p (c i) t -> p c t i", i=GATE_RUN),
                in0=silu[:].rearrange("p t (c i) -> p c t i", i=GATE_RUN),
                in1=normed[group][:].rearrange("p t (c i) -> p c t i", i=GATE_RUN),
                op=ALU.mult,
            )
            gated[group] = h_grouped

        def quantise_gate(group):
            nc.vector.quantize_mx(
                out=h_codes[:, group, :].bitcast(FP8X4),
                scales=h_scales[:, group, :],
                in_=gated[group][:].rearrange("p w t -> p (w t)"),
            )

        out_banks = {}

        def project(n):
            half, group = (n - 8) // PASSES, n % PASSES
            for b in range(CHUNK_COLS // BANK):
                for tt in range(TOKEN_TILES):
                    if group == 0:
                        out_banks[(tt, b)] = psum.tile([P, BANK], F32, name="out_bank", tag="bank")
                    nc.tensor.matmul_mx(
                        out=out_banks[(tt, b)][:],
                        lhsT=h_codes[:, group, tt * P : (tt + 1) * P].bitcast(FP8X4),
                        lhsT_scale=h_scales[:, group, tt * P : (tt + 1) * P],
                        rhs=weight_codes[n][:, b * BANK : (b + 1) * BANK].bitcast(FP8X4),
                        rhs_scale=weight_scales[n][:, b * BANK : (b + 1) * BANK],
                        start=(group == 0),
                        stop=(group == PASSES - 1),
                    )
            if group < PASSES - 1:
                return
            for b in range(CHUNK_COLS // BANK):
                for tt in range(TOKEN_TILES):
                    stage = out_pool.tile([P, BANK], F32, name="stage", tag="stage")
                    if half == HALVES - 1 and tt % 2 == 1:
                        nc.vector.tensor_copy(out=stage[:], in_=out_banks[(tt, b)][:])
                    else:
                        nc.scalar.copy(out=stage[:], in_=out_banks[(tt, b)][:])
                    first = half * CHUNK_COLS + b * BANK
                    nc.sync.dma_start(out=out_rows[tt * P : (tt + 1) * P, first : first + BANK], in_=stage[:])

        waiting = []
        for n in range(N_CHUNKS):
            prepare_chunk(n)
            if n + PREFETCH < N_CHUNKS:
                load_chunk(n + PREFETCH)
            step = n // 2
            if n % 2 == 0 and 2 <= step <= PASSES + 1:
                quantise_gate(step - 2)
            if n % 2 == 1:
                if step < PASSES:
                    normalise(step)
                if 1 <= step <= PASSES:
                    gate(step - 1)
            if n >= 8:
                waiting.append(n)
            if n > 2 * PASSES:
                for ready in waiting:
                    project(ready)
                waiting = []
